import numpy as np
import ml_dtypes


def mxq(x, axis, fmt="e4m3"):
    dtype, down = {"e4m3": (ml_dtypes.float8_e4m3fn, 7), "e5m2": (ml_dtypes.float8_e5m2, 14)}[fmt]
    v = np.moveaxis(np.asarray(x, np.float32).astype(ml_dtypes.bfloat16).astype(np.float64), axis, -1)
    blocks = v.reshape(v.shape[:-1] + (-1, 32))
    amax = np.abs(blocks).max(-1, keepdims=True)
    byte = np.maximum(np.where(amax > 0, np.frexp(amax)[1] - 1 + 127, 0) - down, 1)
    scale = np.exp2(byte - 127.0)
    codes = (blocks / scale).astype(np.float32).astype(dtype).astype(np.float64)
    return np.moveaxis((codes * scale).reshape(v.shape), -1, axis)


WIDE = False


def mx_kscale(k):
    if not WIDE:
        return np.ones(k)
    levels = np.array([10, -10, 5, -5, 0])
    a = np.random.permutation(np.resize(levels, k // 512 * 4)).reshape(k // 512, 4)
    idx = np.arange(k)
    return np.exp2(a[idx // 512, idx % 128 // 32])


BF16 = ml_dtypes.bfloat16


def bf(x):
    return np.asarray(x, np.float32).astype(BF16)


def f64(x):
    return np.asarray(x).astype(np.float64)


B, S, DV, D, H, A = 4, 1024, 1024, 256, 2, 64
LN_EPS = 1e-3


def setup_inputs():
    s = mx_kscale(DV)
    return {
        "attn": bf(np.random.standard_normal((B, H, S, DV)) * 0.4 * s),
        "Wo": bf(np.random.standard_normal((H, DV, D)) * 0.6 / np.sqrt(DV * H) / s[None, :, None]),
        "bo": bf(np.random.standard_normal((H, D)) * 0.12 / np.sqrt(H)),
        "query_inputs": bf(np.random.standard_normal((B, S, D)) * 0.1),
        "gamma": bf(1.0 + 0.1 * np.random.standard_normal(D)),
        "beta": bf(0.1 * np.random.standard_normal(D)),
    }


def reference(attn, Wo, bo, query_inputs, gamma, beta):
    pre = mxq(f64(attn), 3, "e4m3") @ mxq(f64(Wo), 1, "e4m3")
    head_out = np.maximum(pre + f64(bo)[None, :, None, :], 0.0)
    x = f64(query_inputs) + head_out.sum(axis=1)
    mean = x.mean(axis=-1, keepdims=True)
    var = x.var(axis=-1, keepdims=True)
    return f64(gamma) * (x - mean) / np.sqrt(var + LN_EPS) + f64(beta)

@@ -1,0 +1,318 @@
+from contextlib import ExitStack
+
+import concourse.mybir as mybir
+from concourse.masks import make_identity
+
+F32 = mybir.dt.float32
+BF16 = mybir.dt.bfloat16
+U32 = mybir.dt.uint32
+U8 = mybir.dt.uint8
+FP8X4 = mybir.dt.float8_e4m3fn_x4
+ALU = mybir.AluOpType
+ACT = mybir.ActivationFunctionType
+
+B, H, S, DV, D = 4, 2, 1024, 1024, 256
+LN_EPS = 1e-3
+FLOPS = 2 * B * H * S * DV * D
+
+P = 128
+MANUAL = True
+ACCT = True
+XBUFS = 10
+AHEAD = 8
+LQ = 1
+LM = 2
+T_R = ((3, 4), (5, 6))
+T_HS = (6, 7)
+T_TB = (7, 7)
+T_X = (8, 9)
+T_SQ = (9, 10)
+T_E = (10, 11)
+
+
+def ev_on_vector(n, jp):
+    return jp == 1 and (n < 6 or n % 2 == 0)
+
+
+def tile_multiheadattentionunit_pa_t_kernel(tc, attn, Wo, bo, query_inputs, gamma, beta, out):
+    nc = tc.nc
+    with ExitStack() as ctx:
+        const = ctx.enter_context(tc.tile_pool(name="const", bufs=1))
+        xpool = ctx.enter_context(tc.tile_pool(name="xpool", bufs=XBUFS))
+        work = ctx.enter_context(tc.tile_pool(name="work", bufs=3))
+        stat = ctx.enter_context(tc.tile_pool(name="stat", bufs=4))
+        psum = ctx.enter_context(tc.psum_pool(name="psum", bufs=1))
+        if MANUAL:
+            ctx.enter_context(tc.manual_schedule())
+
+        xin = {}
+        grps = {}
+        codes = {}
+        scls = {}
+        pps = {}
+        rs = {}
+        tbs = {}
+        xs = {}
+        outs = {}
+        st = {}
+        qts = {}
+
+        def load(k, parts):
+            b, sg, h = k // 4, (k // 2) % 2, k % 2
+            x = xpool.tile([P, 4, DV], BF16, name="xin", tag="xin")
+            w = DV // parts
+            for i in range(parts):
+                nc.sync.dma_start(
+                    out=x[:, :, i * w:(i + 1) * w],
+                    in_=attn[b, h, sg * 512:(sg + 1) * 512, i * w:(i + 1) * w].rearrange("(p j) k -> p j k", j=4),
+                )
+            xin[k] = x
+
+        def load_q(b):
+            qt = const.tile([P, 2, 4, D], BF16, name="qt%d" % b)
+            nc.sync.dma_start(
+                out=qt[:].rearrange("p s j d -> p s (j d)"),
+                in_=query_inputs[b].rearrange("(s p j) d -> p s (j d)", s=2, j=4),
+            )
+            qts[b] = qt
+
+        gbrow = const.tile([P, 2 * D], BF16, name="gbrow")
+        nc.vector.memset(gbrow[:], 0.0)
+        zb = const.tile([P, P], BF16, name="zb")
+        nc.vector.memset(zb[:], 0.0)
+        nc.scalar.dma_start(out=zb[0:4, :], in_=bo.rearrange("h (c p) -> (h c) p", p=P))
+        nc.scalar.dma_start(out=gbrow[0:1, 0:D], in_=gamma.rearrange("(o d) -> o d", o=1))
+        nc.scalar.dma_start(out=gbrow[0:1, D:2 * D], in_=beta.rearrange("(o d) -> o d", o=1))
+        one_t = const.tile([P, 1], F32, name="one_t")
+        nc.vector.memset(one_t[:], 1.0)
+        eps_t = const.tile([P, 1], F32, name="eps_t")
+        nc.vector.tensor_scalar(out=eps_t[:], in0=one_t[:], scalar1=LN_EPS, scalar2=None, op0=ALU.mult)
+        scr = const.tile([P, 1], F32, name="scr")
+        nc.scalar.activation(out=scr[:], in_=eps_t[:], func=ACT.Sqrt)
+        ident_f = const.tile([P, P], F32, name="ident_f")
+        make_identity(nc, ident_f[:])
+        ident_b = const.tile([P, P], BF16, name="ident_b")
+        make_identity(nc, ident_b[:])
+        ones_b = const.tile([P, P], BF16, name="ones_b")
+        nc.gpsimd.memset(ones_b[:], 1.0)
+
+        wraw = const.tile([P, 4, 4, D], BF16, name="wraw")
+        wcodes = const.tile([P, 4, D], U32, name="wcodes", align_bytes=64)
+        wscl = const.tile([P, 4, D], U8, name="wscl", align_bytes=64)
+        wgrp = const.tile([P, 4, D, 4], BF16, name="wgrp", align_bytes=64)
+        gb = const.tile([P, 2 * D], F32, name="gb")
+        bias_f = const.tile([P, 4], F32, name="bias_f")
+        gam = gb[:, 0:D]
+        bet = gb[:, D:2 * D]
+
+        def load_w(h):
+            nc.sync.dma_start(
+                out=wraw[:, 2 * h:2 * h + 2, :, :].rearrange("p a t c -> p (a t c)").rearrange("p (x y) -> p x y", y=2 * D),
+                in_=Wo[h].rearrange("(g u p e) c -> p (g u) (e c)", g=2, u=2, p=P, e=2),
+            )
+
+        def prep_w(h):
+            for a in (2 * h, 2 * h + 1):
+                src = wraw[:, a, :, :].rearrange("p t c -> p c t")
+                if a % 2 == 0:
+                    nc.vector.tensor_copy(out=wgrp[:, a, :, :], in_=src)
+                else:
+                    nc.scalar.copy(out=wgrp[:, a, :, :], in_=src)
+            for a in (2 * h, 2 * h + 1):
+                nc.vector.quantize_mx(
+                    out=wcodes[:, a, :].bitcast(FP8X4),
+                    scales=wscl[:, a, :],
+                    in_=wgrp[:, a, :, :].rearrange("p c t -> p (c t)"),
+                )
+
+        def const_bias():
+            bps = psum.tile([P, P], BF16, name="bps", tag="tb", bufs=2)
+            nc.tensor.transpose(bps[:], zb[:], ident_b[:])
+            nc.vector.tensor_copy(out=bias_f[:], in_=bps[:, 0:4])
+
+        def const_gb():
+            cps = psum.tile([P, 2 * D], F32, name="cps", tag="tb", bufs=2)
+            nc.tensor.matmul(cps[:], lhsT=ones_b[:], rhs=gbrow[:], start=True, stop=True)
+            nc.vector.tensor_copy(out=gb[:], in_=cps[:])
+
+        def tf_ev(n):
+            k, g = n // 2, n % 2
+            grp = work.tile([P, 512, 2], F32, name="grp", tag="grp", bufs=4, align_bytes=64)
+            grps[n] = grp
+            for jp in range(2):
+                bank = psum.tile([P, 2, 2, P], F32, name="tf", tag="tf", bufs=3)
+                for u in range(2):
+                    for jj in range(2):
+                        c0 = 256 * g + 128 * u
+                        nc.tensor.transpose(
+                            bank[:, u, jj, :],
+                            xin[k][:, 2 * jp + jj, :].bitcast(F32)[:, c0:c0 + 128],
+                            ident_f[:],
+                        )
+                src = bank[:].rearrange("p u j r -> p (j r) u")
+                dst = grp[:, jp * 256:(jp + 1) * 256, :]
+                if ev_on_vector(n, jp):
+                    nc.vector.tensor_copy(out=dst, in_=src)
+                else:
+                    nc.scalar.copy(out=dst, in_=src)
+
+        def quant(n):
+            ac = work.tile([P, 512], U32, name="ac", tag="ac", bufs=4, align_bytes=64)
+            asc = work.tile([P, 512], U8, name="asc", tag="asc", bufs=4, align_bytes=64)
+            nc.vector.quantize_mx(
+                out=ac[:].bitcast(FP8X4),
+                scales=asc[:],
+                in_=grps[n][:].rearrange("p c u -> p (c u)").bitcast(BF16),
+            )
+            codes[n] = ac
+            scls[n] = asc
+
+        def mm(n):
+            k, g = n // 2, n % 2
+            a = 2 * (k % 2) + g
+            for dh in range(2):
+                if g == 0:
+                    pps[(k, dh)] = psum.tile([P, 512], F32, name="pp", tag="pp", bufs=3)
+                nc.tensor.matmul_mx(
+                    out=pps[(k, dh)][:],
+                    lhsT=wcodes[:, a, dh * P:(dh + 1) * P].bitcast(FP8X4),
+                    lhsT_scale=wscl[:, a, dh * P:(dh + 1) * P],
+                    rhs=codes[n][:].bitcast(FP8X4),
+                    rhs_scale=scls[n][:],
+                    start=(g == 0),
+                    stop=(g == 1),
+                )
+
+        def relu(m, h, dh):
+            k = 2 * m + h
+            if h == 0:
+                r = work.tile([P, 512], F32, name="r0", tag="r0", bufs=6)
+            else:
+                r = work.tile([P, 512], F32, name="r1", tag="r1", bufs=4)
+            rs[(m, h, dh)] = r
+            nc.scalar.activation(out=r[:], in_=pps[(k, dh)][:], func=ACT.Relu,
+                                 bias=bias_f[:, 2 * h + dh:2 * h + dh + 1], scale=1.0)
+
+        def headsum(m, dh):
+            nc.vector.tensor_tensor(out=rs[(m, 0, dh)][:], in0=rs[(m, 0, dh)][:], in1=rs[(m, 1, dh)][:], op=ALU.add)
+
+        def tback(m, jp):
+            tb = psum.tile([P, 2, D], F32, name="tb", tag="tb", bufs=2)
+            tbs[(m, jp)] = tb
+            for jj in range(2):
+                j = 2 * jp + jj
+                for dh in range(2):
+                    dst = tb[:, jj, dh * P:(dh + 1) * P]
+                    if ACCT:
+                        for h in range(2):
+                            nc.tensor.matmul(dst, lhsT=rs[(m, h, dh)][:, j * P:(j + 1) * P], rhs=ident_f[:],
+                                             is_transpose=True, start=(h == 0), stop=(h == 1))
+                    else:
+                        nc.tensor.transpose(dst, rs[(m, 0, dh)][:, j * P:(j + 1) * P], ident_f[:])
+
+        def xadd(m, jp):
+            if jp == 0:
+                xs[m] = work.tile([P, 4, D], F32, name="x", tag="x", bufs=3)
+                st[m] = dict(
+                    sums=stat.tile([P, 4], F32, name="sums", tag="sums"),
+                    negm=stat.tile([P, 4], F32, name="negm", tag="negm"),
+                    ss=stat.tile([P, 4], F32, name="ss", tag="ss"),
+                    sd=stat.tile([P, 4], F32, name="sd", tag="sd"),
+                    rstd=stat.tile([P, 4], F32, name="rstd", tag="rstd"),
+                )
+            for j in (2 * jp, 2 * jp + 1):
+                nc.vector.scalar_tensor_tensor(
+                    out=xs[m][:, j, :], in0=tbs[(m, jp)][:, j % 2, :], scalar=0.0,
+                    in1=qts[m // 2][:, m % 2, j, :], op0=ALU.add, op1=ALU.add,
+                    accum_out=st[m]["sums"][:, j:j + 1])
+            nc.vector.tensor_scalar(out=st[m]["negm"][:, 2 * jp:2 * jp + 2], in0=st[m]["sums"][:, 2 * jp:2 * jp + 2],
+                                    scalar1=-1.0 / D, scalar2=None, op0=ALU.mult)
+
+        def sq(m, jp):
+            for j in (2 * jp, 2 * jp + 1):
+                junk = work.tile([P, D], BF16, name="junk", tag="junk", bufs=2)
+                nc.scalar.activation(out=junk[:], in_=xs[m][:, j, :], func=ACT.Square,
+                                     bias=st[m]["negm"][:, j:j + 1], scale=1.0,
+                                     accum_out=st[m]["ss"][:, j:j + 1])
+            nc.scalar.activation(out=st[m]["sd"][:, 2 * jp:2 * jp + 2], in_=st[m]["ss"][:, 2 * jp:2 * jp + 2],
+                                 func=ACT.Sqrt, bias=eps_t[:, 0:1], scale=1.0 / D)
+
+        def norm(m, jp):
+            if jp == 0:
+                outs[m] = work.tile([P, 4, D], F32, name="o", tag="o", bufs=3)
+            nc.vector.reciprocal(out=st[m]["rstd"][:, 2 * jp:2 * jp + 2], in_=st[m]["sd"][:, 2 * jp:2 * jp + 2])
+            for j in (2 * jp, 2 * jp + 1):
+                y = work.tile([P, D], F32, name="y", tag="y", bufs=3)
+                nc.vector.scalar_tensor_tensor(out=y[:], in0=xs[m][:, j, :], scalar=st[m]["negm"][:, j:j + 1],
+                                               in1=gam, op0=ALU.add, op1=ALU.mult)
+                nc.vector.scalar_tensor_tensor(out=outs[m][:, j, :], in0=y[:], scalar=st[m]["rstd"][:, j:j + 1],
+                                               in1=bet, op0=ALU.mult, op1=ALU.add)
+            b, sg = m // 2, m % 2
+            nc.sync.dma_start(
+                out=out[b, sg * 512:(sg + 1) * 512, :].rearrange("(p j) d -> p j d", j=4)[:, 2 * jp:2 * jp + 2, :],
+                in_=outs[m][:, 2 * jp:2 * jp + 2, :],
+            )
+
+        def pair_at(it, t):
+            m, ph = divmod(it - t, 4)
+            return m if (ph == 0 and 0 <= m < 8) else None
+
+        load(0, 2)
+        load_w(0)
+        load(1, 1)
+        load_w(1)
+        load(2, 1)
+        load(3, 1)
+        load_q(0)
+        for k in range(4, AHEAD):
+            load(k, 1)
+            if k == 5:
+                load_q(1)
+        NIT = 32
+        for it in range(NIT + 16):
+            if it % 2 == 0 and it // 2 + AHEAD < 16:
+                load(it // 2 + AHEAD, 1)
+                if it == 0:
+                    load_q(2)
+                if it == 4:
+                    load_q(3)
+            if it == 1:
+                prep_w(0)
+            if it == 2:
+                prep_w(1)
+            if 0 <= it - LQ < NIT:
+                quant(it - LQ)
+            if not ACCT:
+                for dh in range(2):
+                    m = pair_at(it, T_HS[dh])
+                    if m is not None:
+                        headsum(m, dh)
+            if it < NIT:
+                tf_ev(it)
+            if it == 1:
+                const_bias()
+            if it == 4:
+                const_gb()
+            for jp in range(2):
+                m = pair_at(it, T_TB[jp])
+                if m is not None:
+                    tback(m, jp)
+            if 0 <= it - LM < NIT:
+                mm(it - LM)
+            for h in range(2):
+                for dh in range(2):
+                    m = pair_at(it, T_R[h][dh])
+                    if m is not None:
+                        relu(m, h, dh)
+            for jp in range(2):
+                m = pair_at(it, T_X[jp])
+                if m is not None:
+                    xadd(m, jp)
+            for jp in range(2):
+                m = pair_at(it, T_SQ[jp])
+                if m is not None:
+                    sq(m, jp)
+            for jp in range(2):
+                m = pair_at(it, T_E[jp])
+                if m is not None:
+                    norm(m, jp)

@@ -28,6 +28,9 @@ T_TB = (7, 7)
 T_X = (8, 9)
 T_SQ = (9, 10)
 T_E = (10, 11)
+TFB = 2
+D_STEADY = 1
+D_HEAD = 4
 
 
 def ev_on_vector(n, jp):
@@ -135,12 +138,20 @@ def tile_multiheadattentionunit_pa_t_kernel(tc, attn, Wo, bo, query_inputs, gamm
             nc.tensor.matmul(cps[:], lhsT=ones_b[:], rhs=gbrow[:], start=True, stop=True)
             nc.vector.tensor_copy(out=gb[:], in_=cps[:])
 
+        dm = psum.tile([P, 512], F32, name="dm", tag="dm", bufs=1)
+
+        def idle_passes(count):
+            for i in range(count):
+                nc.tensor.matmul_mx(out=dm[:], lhsT=wcodes[:, 0, 0:P].bitcast(FP8X4), lhsT_scale=wscl[:, 0, 0:P],
+                                    rhs=wcodes[:, 0:2, :].rearrange("p a c -> p (a c)").bitcast(FP8X4),
+                                    rhs_scale=wscl[:, 0:2, :].rearrange("p a c -> p (a c)"), start=True, stop=True)
+
         def tf_ev(n):
             k, g = n // 2, n % 2
             grp = work.tile([P, 512, 2], F32, name="grp", tag="grp", bufs=4, align_bytes=64)
             grps[n] = grp
             for jp in range(2):
-                bank = psum.tile([P, 2, 2, P], F32, name="tf", tag="tf", bufs=3)
+                bank = psum.tile([P, 2, 2, P], F32, name="tf", tag="tf", bufs=TFB)
                 for u in range(2):
                     for jj in range(2):
                         c0 = 256 * g + 128 * u
@@ -287,6 +298,8 @@ def tile_multiheadattentionunit_pa_t_kernel(tc, attn, Wo, bo, query_inputs, gamm
                     m = pair_at(it, T_HS[dh])
                     if m is not None:
                         headsum(m, dh)
+            if 2 <= it < 6:
+                idle_passes(D_HEAD)
             if it < NIT:
                 tf_ev(it)
             if it == 1:
@@ -299,6 +312,7 @@ def tile_multiheadattentionunit_pa_t_kernel(tc, attn, Wo, bo, query_inputs, gamm
                     tback(m, jp)
             if 0 <= it - LM < NIT:
                 mm(it - LM)
+                idle_passes(D_STEADY)
             for h in range(2):
                 for dh in range(2):
                     m = pair_at(it, T_R[h][dh])

@@ -16,25 +16,22 @@ LN_EPS = 1e-3
 FLOPS = 2 * B * H * S * DV * D
 
 P = 128
-MANUAL = True
-ACCT = True
-XBUFS = 10
-AHEAD = 8
-LQ = 1
-LM = 2
-T_R = ((3, 4), (5, 6))
-T_HS = (6, 7)
-T_TB = (7, 7)
-T_X = (8, 9)
-T_SQ = (9, 10)
-T_E = (10, 11)
-TFB = 2
-D_STEADY = 1
-D_HEAD = 4
+NSTEP = 32
+XBUFS = 18
+AHEAD = 14
+L_TB = 6
+V_HEAD = 6
+V_EVERY = 100
+V_LAST = 28
+Q_AT = (4, 10, 18, 26)
 
 
-def ev_on_vector(n, jp):
-    return jp == 1 and (n < 6 or n % 2 == 0)
+def ev_on_vector(n):
+    if n < V_HEAD:
+        return True
+    if n >= V_LAST:
+        return False
+    return n % V_EVERY == 0
 
 
 def tile_multiheadattentionunit_pa_t_kernel(tc, attn, Wo, bo, query_inputs, gamma, beta, out):
@@ -43,39 +40,38 @@ def tile_multiheadattentionunit_pa_t_kernel(tc, attn, Wo, bo, query_inputs, gamm
         const = ctx.enter_context(tc.tile_pool(name="const", bufs=1))
         xpool = ctx.enter_context(tc.tile_pool(name="xpool", bufs=XBUFS))
         work = ctx.enter_context(tc.tile_pool(name="work", bufs=3))
-        stat = ctx.enter_context(tc.tile_pool(name="stat", bufs=4))
+        stat = ctx.enter_context(tc.tile_pool(name="stat", bufs=8))
         psum = ctx.enter_context(tc.psum_pool(name="psum", bufs=1))
-        if MANUAL:
-            ctx.enter_context(tc.manual_schedule())
+        ctx.enter_context(tc.manual_schedule())
 
         xin = {}
         grps = {}
+        banks = {}
         codes = {}
         scls = {}
         pps = {}
         rs = {}
         tbs = {}
-        xs = {}
+        ys = {}
         outs = {}
         st = {}
         qts = {}
 
-        def load(k, parts):
-            b, sg, h = k // 4, (k // 2) % 2, k % 2
-            x = xpool.tile([P, 4, DV], BF16, name="xin", tag="xin")
+        def load(s, parts):
+            blk, h = s // 2, s % 2
+            x = xpool.tile([P, 2, DV], BF16, name="xin", tag="xin")
+            r0 = (blk % 4) * 256
+            src = attn[blk // 4, h, r0:r0 + 256, :].rearrange("(p j) k -> p j k", j=2)
             w = DV // parts
             for i in range(parts):
-                nc.sync.dma_start(
-                    out=x[:, :, i * w:(i + 1) * w],
-                    in_=attn[b, h, sg * 512:(sg + 1) * 512, i * w:(i + 1) * w].rearrange("(p j) k -> p j k", j=4),
-                )
-            xin[k] = x
+                nc.sync.dma_start(out=x[:, :, i * w:(i + 1) * w], in_=src[:, :, i * w:(i + 1) * w])
+            xin[s] = x
 
         def load_q(b):
-            qt = const.tile([P, 2, 4, D], BF16, name="qt%d" % b)
+            qt = const.tile([P, 4, 2, D], BF16, name="qt%d" % b)
             nc.sync.dma_start(
                 out=qt[:].rearrange("p s j d -> p s (j d)"),
-                in_=query_inputs[b].rearrange("(s p j) d -> p s (j d)", s=2, j=4),
+                in_=query_inputs[b].rearrange("(s p j) d -> p s (j d)", s=4, j=2),
             )
             qts[b] = qt
 
@@ -114,19 +110,19 @@ def tile_multiheadattentionunit_pa_t_kernel(tc, attn, Wo, bo, query_inputs, gamm
                 in_=Wo[h].rearrange("(g u p e) c -> p (g u) (e c)", g=2, u=2, p=P, e=2),
             )
 
-        def prep_w(h):
-            for a in (2 * h, 2 * h + 1):
-                src = wraw[:, a, :, :].rearrange("p t c -> p c t")
-                if a % 2 == 0:
-                    nc.vector.tensor_copy(out=wgrp[:, a, :, :], in_=src)
-                else:
-                    nc.scalar.copy(out=wgrp[:, a, :, :], in_=src)
-            for a in (2 * h, 2 * h + 1):
-                nc.vector.quantize_mx(
-                    out=wcodes[:, a, :].bitcast(FP8X4),
-                    scales=wscl[:, a, :],
-                    in_=wgrp[:, a, :, :].rearrange("p c t -> p (c t)"),
-                )
+        def regroup_w(a, eng):
+            src = wraw[:, a, :, :].rearrange("p t c -> p c t")
+            if eng == "v":
+                nc.vector.tensor_copy(out=wgrp[:, a, :, :], in_=src)
+            else:
+                nc.scalar.copy(out=wgrp[:, a, :, :], in_=src)
+
+        def quant_w(a):
+            nc.vector.quantize_mx(
+                out=wcodes[:, a, :].bitcast(FP8X4),
+                scales=wscl[:, a, :],
+                in_=wgrp[:, a, :, :].rearrange("p c t -> p (c t)"),
+            )
 
         def const_bias():
             bps = psum.tile([P, P], BF16, name="bps", tag="tb", bufs=2)
@@ -138,195 +134,182 @@ def tile_multiheadattentionunit_pa_t_kernel(tc, attn, Wo, bo, query_inputs, gamm
             nc.tensor.matmul(cps[:], lhsT=ones_b[:], rhs=gbrow[:], start=True, stop=True)
             nc.vector.tensor_copy(out=gb[:], in_=cps[:])
 
-        dm = psum.tile([P, 512], F32, name="dm", tag="dm", bufs=1)
-
-        def idle_passes(count):
-            for i in range(count):
-                nc.tensor.matmul_mx(out=dm[:], lhsT=wcodes[:, 0, 0:P].bitcast(FP8X4), lhsT_scale=wscl[:, 0, 0:P],
-                                    rhs=wcodes[:, 0:2, :].rearrange("p a c -> p (a c)").bitcast(FP8X4),
-                                    rhs_scale=wscl[:, 0:2, :].rearrange("p a c -> p (a c)"), start=True, stop=True)
-
-        def tf_ev(n):
-            k, g = n // 2, n % 2
-            grp = work.tile([P, 512, 2], F32, name="grp", tag="grp", bufs=4, align_bytes=64)
-            grps[n] = grp
-            for jp in range(2):
-                bank = psum.tile([P, 2, 2, P], F32, name="tf", tag="tf", bufs=TFB)
+        def tf(s):
+            grps[s] = work.tile([P, 512, 2], F32, name="grp", tag="grp", bufs=4, align_bytes=64)
+            for g in range(2):
+                bank = psum.tile([P, 2, 2, P], F32, name="tf", tag="tf", bufs=3)
+                banks[(s, g)] = bank
                 for u in range(2):
                     for jj in range(2):
                         c0 = 256 * g + 128 * u
-                        nc.tensor.transpose(
-                            bank[:, u, jj, :],
-                            xin[k][:, 2 * jp + jj, :].bitcast(F32)[:, c0:c0 + 128],
-                            ident_f[:],
-                        )
-                src = bank[:].rearrange("p u j r -> p (j r) u")
-                dst = grp[:, jp * 256:(jp + 1) * 256, :]
-                if ev_on_vector(n, jp):
-                    nc.vector.tensor_copy(out=dst, in_=src)
-                else:
-                    nc.scalar.copy(out=dst, in_=src)
+                        nc.tensor.transpose(bank[:, u, jj, :], xin[s][:, jj, :].bitcast(F32)[:, c0:c0 + 128], ident_f[:])
 
-        def quant(n):
+        def evac(s, g, on_vector):
+            src = banks[(s, g)][:].rearrange("p u j r -> p (j r) u")
+            dst = grps[s][:, g * 256:(g + 1) * 256, :]
+            if on_vector:
+                nc.vector.tensor_copy(out=dst, in_=src)
+            else:
+                nc.scalar.copy(out=dst, in_=src)
+
+        def quant(s):
             ac = work.tile([P, 512], U32, name="ac", tag="ac", bufs=4, align_bytes=64)
             asc = work.tile([P, 512], U8, name="asc", tag="asc", bufs=4, align_bytes=64)
             nc.vector.quantize_mx(
                 out=ac[:].bitcast(FP8X4),
                 scales=asc[:],
-                in_=grps[n][:].rearrange("p c u -> p (c u)").bitcast(BF16),
+                in_=grps[s][:].rearrange("p c u -> p (c u)").bitcast(BF16),
             )
-            codes[n] = ac
-            scls[n] = asc
+            codes[s] = ac
+            scls[s] = asc
 
-        def mm(n):
-            k, g = n // 2, n % 2
-            a = 2 * (k % 2) + g
+        def mm(s):
+            h = s % 2
+            pps[s] = psum.tile([P, 2, 256], F32, name="pp", tag=("tf" if s == NSTEP - 1 else "pp"), bufs=3)
             for dh in range(2):
-                if g == 0:
-                    pps[(k, dh)] = psum.tile([P, 512], F32, name="pp", tag="pp", bufs=3)
-                nc.tensor.matmul_mx(
-                    out=pps[(k, dh)][:],
-                    lhsT=wcodes[:, a, dh * P:(dh + 1) * P].bitcast(FP8X4),
-                    lhsT_scale=wscl[:, a, dh * P:(dh + 1) * P],
-                    rhs=codes[n][:].bitcast(FP8X4),
-                    rhs_scale=scls[n][:],
-                    start=(g == 0),
-                    stop=(g == 1),
-                )
+                for g in range(2):
+                    nc.tensor.matmul_mx(
+                        out=pps[s][:, dh, :],
+                        lhsT=wcodes[:, 2 * h + g, dh * P:(dh + 1) * P].bitcast(FP8X4),
+                        lhsT_scale=wscl[:, 2 * h + g, dh * P:(dh + 1) * P],
+                        rhs=codes[s][:, g * 256:(g + 1) * 256].bitcast(FP8X4),
+                        rhs_scale=scls[s][:, g * 256:(g + 1) * 256],
+                        start=(g == 0),
+                        stop=(g == 1),
+                    )
 
-        def relu(m, h, dh):
-            k = 2 * m + h
-            if h == 0:
-                r = work.tile([P, 512], F32, name="r0", tag="r0", bufs=6)
-            else:
-                r = work.tile([P, 512], F32, name="r1", tag="r1", bufs=4)
-            rs[(m, h, dh)] = r
-            nc.scalar.activation(out=r[:], in_=pps[(k, dh)][:], func=ACT.Relu,
-                                 bias=bias_f[:, 2 * h + dh:2 * h + dh + 1], scale=1.0)
+        def relu(s):
+            h = s % 2
+            r = work.tile([P, 2, 256], F32, name="r", tag="r", bufs=6)
+            rs[s] = r
+            for dh in (1, 0):
+                nc.scalar.activation(out=r[:, dh, :], in_=pps[s][:, dh, :], func=ACT.Relu,
+                                     bias=bias_f[:, 2 * h + dh:2 * h + dh + 1], scale=1.0)
 
-        def headsum(m, dh):
-            nc.vector.tensor_tensor(out=rs[(m, 0, dh)][:], in0=rs[(m, 0, dh)][:], in1=rs[(m, 1, dh)][:], op=ALU.add)
+        def tback(a):
+            blk, jj = a // 2, a % 2
+            tag = {28: "tf", 29: "tf", 30: "pp", 31: "pp"}.get(a, "tb")
+            tb = psum.tile([P, 2 * D], F32, name="tb", tag=tag, bufs=(2 if tag == "tb" else 3))
+            tbs[a] = tb
+            for dh in range(2):
+                dst = tb[:, dh * P:(dh + 1) * P]
+                nc.tensor.matmul(dst, lhsT=ident_b[:], rhs=qts[blk // 4][:, blk % 4, jj, dh * P:(dh + 1) * P],
+                                 start=True, stop=False)
+                for h in range(2):
+                    nc.tensor.matmul(dst, lhsT=rs[2 * blk + h][:, dh, jj * P:(jj + 1) * P],
+                                     rhs=ident_f[:], is_transpose=True, start=False, stop=(h == 1))
 
-        def tback(m, jp):
-            tb = psum.tile([P, 2, D], F32, name="tb", tag="tb", bufs=2)
-            tbs[(m, jp)] = tb
-            for jj in range(2):
-                j = 2 * jp + jj
-                for dh in range(2):
-                    dst = tb[:, jj, dh * P:(dh + 1) * P]
-                    if ACCT:
-                        for h in range(2):
-                            nc.tensor.matmul(dst, lhsT=rs[(m, h, dh)][:, j * P:(j + 1) * P], rhs=ident_f[:],
-                                             is_transpose=True, start=(h == 0), stop=(h == 1))
-                    else:
-                        nc.tensor.transpose(dst, rs[(m, 0, dh)][:, j * P:(j + 1) * P], ident_f[:])
-
-        def xadd(m, jp):
-            if jp == 0:
-                xs[m] = work.tile([P, 4, D], F32, name="x", tag="x", bufs=3)
-                st[m] = dict(
-                    sums=stat.tile([P, 4], F32, name="sums", tag="sums"),
-                    negm=stat.tile([P, 4], F32, name="negm", tag="negm"),
-                    ss=stat.tile([P, 4], F32, name="ss", tag="ss"),
-                    sd=stat.tile([P, 4], F32, name="sd", tag="sd"),
-                    rstd=stat.tile([P, 4], F32, name="rstd", tag="rstd"),
-                )
-            for j in (2 * jp, 2 * jp + 1):
-                nc.vector.scalar_tensor_tensor(
-                    out=xs[m][:, j, :], in0=tbs[(m, jp)][:, j % 2, :], scalar=0.0,
-                    in1=qts[m // 2][:, m % 2, j, :], op0=ALU.add, op1=ALU.add,
-                    accum_out=st[m]["sums"][:, j:j + 1])
-            nc.vector.tensor_scalar(out=st[m]["negm"][:, 2 * jp:2 * jp + 2], in0=st[m]["sums"][:, 2 * jp:2 * jp + 2],
-                                    scalar1=-1.0 / D, scalar2=None, op0=ALU.mult)
-
-        def sq(m, jp):
-            for j in (2 * jp, 2 * jp + 1):
-                junk = work.tile([P, D], BF16, name="junk", tag="junk", bufs=2)
-                nc.scalar.activation(out=junk[:], in_=xs[m][:, j, :], func=ACT.Square,
-                                     bias=st[m]["negm"][:, j:j + 1], scale=1.0,
-                                     accum_out=st[m]["ss"][:, j:j + 1])
-            nc.scalar.activation(out=st[m]["sd"][:, 2 * jp:2 * jp + 2], in_=st[m]["ss"][:, 2 * jp:2 * jp + 2],
-                                 func=ACT.Sqrt, bias=eps_t[:, 0:1], scale=1.0 / D)
-
-        def norm(m, jp):
-            if jp == 0:
-                outs[m] = work.tile([P, 4, D], F32, name="o", tag="o", bufs=3)
-            nc.vector.reciprocal(out=st[m]["rstd"][:, 2 * jp:2 * jp + 2], in_=st[m]["sd"][:, 2 * jp:2 * jp + 2])
-            for j in (2 * jp, 2 * jp + 1):
-                y = work.tile([P, D], F32, name="y", tag="y", bufs=3)
-                nc.vector.scalar_tensor_tensor(out=y[:], in0=xs[m][:, j, :], scalar=st[m]["negm"][:, j:j + 1],
-                                               in1=gam, op0=ALU.add, op1=ALU.mult)
-                nc.vector.scalar_tensor_tensor(out=outs[m][:, j, :], in0=y[:], scalar=st[m]["rstd"][:, j:j + 1],
-                                               in1=bet, op0=ALU.mult, op1=ALU.add)
-            b, sg = m // 2, m % 2
-            nc.sync.dma_start(
-                out=out[b, sg * 512:(sg + 1) * 512, :].rearrange("(p j) d -> p j d", j=4)[:, 2 * jp:2 * jp + 2, :],
-                in_=outs[m][:, 2 * jp:2 * jp + 2, :],
+        def stats(a):
+            st[a] = dict(
+                bn=stat.tile([P, 6], F32, name="bn", tag="bn"),
+                mv=stat.tile([P, 2], F32, name="mv", tag="mv"),
+                sd=stat.tile([P, 1], F32, name="sd", tag="sd"),
+                rstd=stat.tile([P, 1], F32, name="rstd", tag="rstd"),
             )
+            nc.vector.bn_stats(out=st[a]["bn"][:], in_=tbs[a][:, 0:D])
 
-        def pair_at(it, t):
-            m, ph = divmod(it - t, 4)
-            return m if (ph == 0 and 0 <= m < 8) else None
+        def aggr(a):
+            nc.vector.bn_aggr(out=st[a]["mv"][:], in_=st[a]["bn"][:])
+
+        def sqrt(a):
+            nc.scalar.activation(out=st[a]["sd"][:], in_=st[a]["mv"][:, 1:2], func=ACT.Sqrt, bias=eps_t[:, 0:1], scale=1.0)
+
+        def recip(a):
+            nc.vector.reciprocal(out=st[a]["rstd"][:], in_=st[a]["sd"][:])
+
+        def norm1(a):
+            ys[a] = work.tile([P, D], F32, name="y", tag="y", bufs=4)
+            nc.vector.scalar_tensor_tensor(out=ys[a][:], in0=tbs[a][:, 0:D], scalar=st[a]["mv"][:, 0:1], in1=gam,
+                                           op0=ALU.subtract, op1=ALU.mult)
+
+        def norm2(a):
+            blk, jj = a // 2, a % 2
+            if jj == 0:
+                outs[blk] = work.tile([P, 2, D], F32, name="o", tag="o", bufs=8)
+            o = outs[blk]
+            nc.vector.scalar_tensor_tensor(out=o[:, jj, :], in0=ys[a][:], scalar=st[a]["rstd"][:], in1=bet,
+                                           op0=ALU.mult, op1=ALU.add)
+            r0 = (blk % 4) * 256
+            dst = out[blk // 4, r0:r0 + 256, :].rearrange("(p j) d -> p j d", j=2)
+            if blk == 15:
+                nc.sync.dma_start(out=dst[:, jj:jj + 1, :], in_=o[:, jj:jj + 1, :])
+            elif jj == 1:
+                nc.sync.dma_start(out=dst, in_=o[:])
 
         load(0, 2)
         load_w(0)
         load(1, 1)
         load_w(1)
-        load(2, 1)
-        load(3, 1)
-        load_q(0)
-        for k in range(4, AHEAD):
-            load(k, 1)
-            if k == 5:
-                load_q(1)
-        NIT = 32
-        for it in range(NIT + 16):
-            if it % 2 == 0 and it // 2 + AHEAD < 16:
-                load(it // 2 + AHEAD, 1)
-                if it == 0:
-                    load_q(2)
-                if it == 4:
-                    load_q(3)
-            if it == 1:
-                prep_w(0)
-            if it == 2:
-                prep_w(1)
-            if 0 <= it - LQ < NIT:
-                quant(it - LQ)
-            if not ACCT:
-                for dh in range(2):
-                    m = pair_at(it, T_HS[dh])
-                    if m is not None:
-                        headsum(m, dh)
-            if 2 <= it < 6:
-                idle_passes(D_HEAD)
-            if it < NIT:
-                tf_ev(it)
-            if it == 1:
+        for s in range(2, AHEAD):
+            load(s, 1)
+            if s in Q_AT:
+                load_q(Q_AT.index(s))
+
+        def rt(v):
+            return 0 <= v < 32
+
+        def ln_round(a):
+            if rt(a):
+                stats(a)
+            if rt(a - 1):
+                norm1(a - 1)
+            if rt(a):
+                aggr(a)
+            if rt(a - 2):
+                norm2(a - 2)
+            if rt(a - 1):
+                recip(a - 1)
+
+        for it in range(NSTEP):
+            if it + AHEAD < NSTEP:
+                load(it + AHEAD, 1)
+                if it + AHEAD in Q_AT:
+                    load_q(Q_AT.index(it + AHEAD))
+            t0 = it - L_TB
+            if rt(t0 - 1):
+                sqrt(t0 - 1)
+            tf(it)
+            evac(it, 0, False)
+            if rt(t0):
+                tback(t0)
+            if it == 0:
+                evac(it, 1, True)
+                regroup_w(0, "v")
+                regroup_w(1, "s")
                 const_bias()
+            if it == NSTEP - 1:
+                evac(it, 1, False)
+            if it - 4 >= 0:
+                relu(it - 4)
+            if it >= 1:
+                quant(it - 1)
+            if it == 1:
+                quant_w(0)
+                quant_w(1)
+                evac(it, 1, True)
+                regroup_w(2, "v")
+                regroup_w(3, "s")
+            if it == 2:
+                quant_w(2)
+                quant_w(3)
             if it == 4:
                 const_gb()
-            for jp in range(2):
-                m = pair_at(it, T_TB[jp])
-                if m is not None:
-                    tback(m, jp)
-            if 0 <= it - LM < NIT:
-                mm(it - LM)
-                idle_passes(D_STEADY)
-            for h in range(2):
-                for dh in range(2):
-                    m = pair_at(it, T_R[h][dh])
-                    if m is not None:
-                        relu(m, h, dh)
-            for jp in range(2):
-                m = pair_at(it, T_X[jp])
-                if m is not None:
-                    xadd(m, jp)
-            for jp in range(2):
-                m = pair_at(it, T_SQ[jp])
-                if m is not None:
-                    sq(m, jp)
-            for jp in range(2):
-                m = pair_at(it, T_E[jp])
-                if m is not None:
-                    norm(m, jp)
+            if it % 2 == 1 and it >= 3:
+                mm(it - 3)
+                mm(it - 2)
+            ln_round(t0)
+            if 2 <= it < NSTEP - 1:
+                evac(it, 1, ev_on_vector(it))
+        quant(NSTEP - 1)
+        mm(NSTEP - 2)
+        mm(NSTEP - 1)
+        for s in range(NSTEP - 4, NSTEP):
+            relu(s)
+            if s == NSTEP - 4:
+                sqrt(NSTEP - L_TB - 1)
+        for a in range(NSTEP - L_TB, NSTEP + 3):
+            if rt(a):
+                tback(a)
+            ln_round(a)
+            if rt(a):
+                sqrt(a)

@@ -17,21 +17,11 @@ FLOPS = 2 * B * H * S * DV * D
 
 P = 128
 NSTEP = 32
+NBLK = 16
 XBUFS = 18
 AHEAD = 14
-L_TB = 6
-V_HEAD = 6
-V_EVERY = 100
-V_LAST = 28
-Q_AT = (4, 10, 18, 26)
-
-
-def ev_on_vector(n):
-    if n < V_HEAD:
-        return True
-    if n >= V_LAST:
-        return False
-    return n % V_EVERY == 0
+V_EV = ()
+Q_LEAD = 3
 
 
 def tile_multiheadattentionunit_pa_t_kernel(tc, attn, Wo, bo, query_inputs, gamma, beta, out):
@@ -40,7 +30,7 @@ def tile_multiheadattentionunit_pa_t_kernel(tc, attn, Wo, bo, query_inputs, gamm
         const = ctx.enter_context(tc.tile_pool(name="const", bufs=1))
         xpool = ctx.enter_context(tc.tile_pool(name="xpool", bufs=XBUFS))
         work = ctx.enter_context(tc.tile_pool(name="work", bufs=3))
-        stat = ctx.enter_context(tc.tile_pool(name="stat", bufs=8))
+        stat = ctx.enter_context(tc.tile_pool(name="stat", bufs=6))
         psum = ctx.enter_context(tc.psum_pool(name="psum", bufs=1))
         ctx.enter_context(tc.manual_schedule())
 
@@ -67,13 +57,13 @@ def tile_multiheadattentionunit_pa_t_kernel(tc, attn, Wo, bo, query_inputs, gamm
                 nc.sync.dma_start(out=x[:, :, i * w:(i + 1) * w], in_=src[:, :, i * w:(i + 1) * w])
             xin[s] = x
 
-        def load_q(b):
-            qt = const.tile([P, 4, 2, D], BF16, name="qt%d" % b)
-            nc.sync.dma_start(
-                out=qt[:].rearrange("p s j d -> p s (j d)"),
-                in_=query_inputs[b].rearrange("(s p j) d -> p s (j d)", s=4, j=2),
-            )
-            qts[b] = qt
+        def load_q(blk):
+            qt = work.tile([P, 2, D], BF16, name="qt", tag="qt", bufs=10)
+            r0 = (blk % 4) * 256
+            nc.sync.dma_start(out=qt[:], in_=query_inputs[blk // 4, r0:r0 + 256, :].rearrange("(p j) d -> p j d", j=2))
+            qts[blk] = qt
+
+        load(0, 2)
 
         gbrow = const.tile([P, 2 * D], BF16, name="gbrow")
         nc.vector.memset(gbrow[:], 0.0)
@@ -124,9 +114,12 @@ def tile_multiheadattentionunit_pa_t_kernel(tc, attn, Wo, bo, query_inputs, gamm
                 in_=wgrp[:, a, :, :].rearrange("p c t -> p (c t)"),
             )
 
-        def const_bias():
-            bps = psum.tile([P, P], BF16, name="bps", tag="tb", bufs=2)
+        bps = psum.tile([P, P], BF16, name="bps", tag="tb", bufs=2)
+
+        def const_bias_t():
             nc.tensor.transpose(bps[:], zb[:], ident_b[:])
+
+        def const_bias_c():
             nc.vector.tensor_copy(out=bias_f[:], in_=bps[:, 0:4])
 
         def const_gb():
@@ -137,7 +130,7 @@ def tile_multiheadattentionunit_pa_t_kernel(tc, attn, Wo, bo, query_inputs, gamm
         def tf(s):
             grps[s] = work.tile([P, 512, 2], F32, name="grp", tag="grp", bufs=4, align_bytes=64)
             for g in range(2):
-                bank = psum.tile([P, 2, 2, P], F32, name="tf", tag="tf", bufs=3)
+                bank = psum.tile([P, 2, 2, P], F32, name="tf", tag="tf", bufs=4)
                 banks[(s, g)] = bank
                 for u in range(2):
                     for jj in range(2):
@@ -153,8 +146,8 @@ def tile_multiheadattentionunit_pa_t_kernel(tc, attn, Wo, bo, query_inputs, gamm
                 nc.scalar.copy(out=dst, in_=src)
 
         def quant(s):
-            ac = work.tile([P, 512], U32, name="ac", tag="ac", bufs=4, align_bytes=64)
-            asc = work.tile([P, 512], U8, name="asc", tag="asc", bufs=4, align_bytes=64)
+            ac = work.tile([P, 512], U32, name="ac", tag="ac", bufs=5, align_bytes=64)
+            asc = work.tile([P, 512], U8, name="asc", tag="asc", bufs=5, align_bytes=64)
             nc.vector.quantize_mx(
                 out=ac[:].bitcast(FP8X4),
                 scales=asc[:],
@@ -165,7 +158,10 @@ def tile_multiheadattentionunit_pa_t_kernel(tc, attn, Wo, bo, query_inputs, gamm
 
         def mm(s):
             h = s % 2
-            pps[s] = psum.tile([P, 2, 256], F32, name="pp", tag=("tf" if s == NSTEP - 1 else "pp"), bufs=3)
+            if s >= NSTEP - 2:
+                pps[s] = psum.tile([P, 2, 256], F32, name="pp", tag="tf", bufs=4)
+            else:
+                pps[s] = psum.tile([P, 2, 256], F32, name="pp", tag="pp", bufs=2)
             for dh in range(2):
                 for g in range(2):
                     nc.tensor.matmul_mx(
@@ -186,130 +182,150 @@ def tile_multiheadattentionunit_pa_t_kernel(tc, attn, Wo, bo, query_inputs, gamm
                 nc.scalar.activation(out=r[:, dh, :], in_=pps[s][:, dh, :], func=ACT.Relu,
                                      bias=bias_f[:, 2 * h + dh:2 * h + dh + 1], scale=1.0)
 
-        def tback(a):
-            blk, jj = a // 2, a % 2
-            tag = {28: "tf", 29: "tf", 30: "pp", 31: "pp"}.get(a, "tb")
-            tb = psum.tile([P, 2 * D], F32, name="tb", tag=tag, bufs=(2 if tag == "tb" else 3))
-            tbs[a] = tb
-            for dh in range(2):
-                dst = tb[:, dh * P:(dh + 1) * P]
-                nc.tensor.matmul(dst, lhsT=ident_b[:], rhs=qts[blk // 4][:, blk % 4, jj, dh * P:(dh + 1) * P],
-                                 start=True, stop=False)
-                for h in range(2):
-                    nc.tensor.matmul(dst, lhsT=rs[2 * blk + h][:, dh, jj * P:(jj + 1) * P],
-                                     rhs=ident_f[:], is_transpose=True, start=False, stop=(h == 1))
+        def tback(blk):
+            tb = psum.tile([P, 2, D], F32, name="tb", tag="tb", bufs=2)
+            tbs[blk] = tb
+            nc.tensor.matmul(tb[:].rearrange("p j d -> p (j d)"), lhsT=ident_b[:],
+                             rhs=qts[blk][:].rearrange("p j d -> p (j d)"), start=True, stop=False)
+            for jj in range(2):
+                for dh in range(2):
+                    for h in range(2):
+                        nc.tensor.matmul(tb[:, jj, dh * P:(dh + 1) * P], lhsT=rs[2 * blk + h][:, dh, jj * P:(jj + 1) * P],
+                                         rhs=ident_f[:], is_transpose=True, start=False,
+                                         stop=(jj == 1 and dh == 1 and h == 1))
 
-        def stats(a):
-            st[a] = dict(
-                bn=stat.tile([P, 6], F32, name="bn", tag="bn"),
-                mv=stat.tile([P, 2], F32, name="mv", tag="mv"),
-                sd=stat.tile([P, 1], F32, name="sd", tag="sd"),
-                rstd=stat.tile([P, 1], F32, name="rstd", tag="rstd"),
+        def stats(blk):
+            st[blk] = dict(
+                bn=stat.tile([P, 2, 6], F32, name="bn", tag="bn"),
+                mv=stat.tile([P, 2, 2], F32, name="mv", tag="mv"),
+                sd=stat.tile([P, 2], F32, name="sd", tag="sd"),
+                rstd=stat.tile([P, 2], F32, name="rstd", tag="rstd"),
             )
-            nc.vector.bn_stats(out=st[a]["bn"][:], in_=tbs[a][:, 0:D])
+            for jj in (1, 0):
+                nc.vector.bn_stats(out=st[blk]["bn"][:, jj, :], in_=tbs[blk][:, jj, :])
 
-        def aggr(a):
-            nc.vector.bn_aggr(out=st[a]["mv"][:], in_=st[a]["bn"][:])
+        def aggr(blk):
+            for jj in (1, 0):
+                nc.vector.bn_aggr(out=st[blk]["mv"][:, jj, :], in_=st[blk]["bn"][:, jj, :])
 
-        def sqrt(a):
-            nc.scalar.activation(out=st[a]["sd"][:], in_=st[a]["mv"][:, 1:2], func=ACT.Sqrt, bias=eps_t[:, 0:1], scale=1.0)
+        def sqrt(blk):
+            nc.scalar.activation(out=st[blk]["sd"][:], in_=st[blk]["mv"][:, :, 1], func=ACT.Sqrt, bias=eps_t[:, 0:1], scale=1.0)
 
-        def recip(a):
-            nc.vector.reciprocal(out=st[a]["rstd"][:], in_=st[a]["sd"][:])
+        def recip(blk):
+            nc.vector.reciprocal(out=st[blk]["rstd"][:], in_=st[blk]["sd"][:])
 
-        def norm1(a):
-            ys[a] = work.tile([P, D], F32, name="y", tag="y", bufs=4)
-            nc.vector.scalar_tensor_tensor(out=ys[a][:], in0=tbs[a][:, 0:D], scalar=st[a]["mv"][:, 0:1], in1=gam,
-                                           op0=ALU.subtract, op1=ALU.mult)
+        def norm1(blk):
+            ys[blk] = work.tile([P, 2, D], F32, name="y", tag="y", bufs=3)
+            for jj in range(2):
+                nc.vector.scalar_tensor_tensor(out=ys[blk][:, jj, :], in0=tbs[blk][:, jj, :], scalar=st[blk]["mv"][:, jj, 0:1],
+                                               in1=gam, op0=ALU.subtract, op1=ALU.mult)
 
-        def norm2(a):
-            blk, jj = a // 2, a % 2
-            if jj == 0:
-                outs[blk] = work.tile([P, 2, D], F32, name="o", tag="o", bufs=8)
-            o = outs[blk]
-            nc.vector.scalar_tensor_tensor(out=o[:, jj, :], in0=ys[a][:], scalar=st[a]["rstd"][:], in1=bet,
-                                           op0=ALU.mult, op1=ALU.add)
+        def norm2(blk):
+            o = work.tile([P, 2, D], F32, name="o", tag="o", bufs=8)
             r0 = (blk % 4) * 256
             dst = out[blk // 4, r0:r0 + 256, :].rearrange("(p j) d -> p j d", j=2)
-            if blk == 15:
-                nc.sync.dma_start(out=dst[:, jj:jj + 1, :], in_=o[:, jj:jj + 1, :])
-            elif jj == 1:
+            for jj in range(2):
+                nc.vector.scalar_tensor_tensor(out=o[:, jj, :], in0=ys[blk][:, jj, :], scalar=st[blk]["rstd"][:, jj:jj + 1],
+                                               in1=bet, op0=ALU.mult, op1=ALU.add)
+                if blk == NBLK - 1:
+                    nc.sync.dma_start(out=dst[:, jj:jj + 1, :], in_=o[:, jj:jj + 1, :])
+            if blk < NBLK - 1:
                 nc.sync.dma_start(out=dst, in_=o[:])
 
-        load(0, 2)
+        def ok(b):
+            return 0 <= b < NBLK
+
+        def loads_for(s):
+            load(s, 1)
+            if s % 2 == 1 and ok((s - Q_LEAD) // 2):
+                load_q((s - Q_LEAD) // 2)
+
         load_w(0)
         load(1, 1)
         load_w(1)
         for s in range(2, AHEAD):
-            load(s, 1)
-            if s in Q_AT:
-                load_q(Q_AT.index(s))
+            loads_for(s)
 
-        def rt(v):
-            return 0 <= v < 32
-
-        def ln_round(a):
-            if rt(a):
-                stats(a)
-            if rt(a - 1):
-                norm1(a - 1)
-            if rt(a):
-                aggr(a)
-            if rt(a - 2):
-                norm2(a - 2)
-            if rt(a - 1):
-                recip(a - 1)
-
-        for it in range(NSTEP):
-            if it + AHEAD < NSTEP:
-                load(it + AHEAD, 1)
-                if it + AHEAD in Q_AT:
-                    load_q(Q_AT.index(it + AHEAD))
-            t0 = it - L_TB
-            if rt(t0 - 1):
-                sqrt(t0 - 1)
-            tf(it)
-            evac(it, 0, False)
-            if rt(t0):
-                tback(t0)
-            if it == 0:
-                evac(it, 1, True)
-                regroup_w(0, "v")
-                regroup_w(1, "s")
-                const_bias()
-            if it == NSTEP - 1:
-                evac(it, 1, False)
-            if it - 4 >= 0:
-                relu(it - 4)
-            if it >= 1:
-                quant(it - 1)
-            if it == 1:
-                quant_w(0)
-                quant_w(1)
-                evac(it, 1, True)
-                regroup_w(2, "v")
-                regroup_w(3, "s")
-            if it == 2:
+        for k in range(NBLK):
+            e, o = 2 * k, 2 * k + 1
+            for s in (e + AHEAD, o + AHEAD):
+                if s < NSTEP:
+                    loads_for(s)
+                elif s % 2 == 1 and ok((s - Q_LEAD) // 2):
+                    load_q((s - Q_LEAD) // 2)
+            if ok(k - 2):
+                relu(e - 4)
+                relu(o - 4)
+            if ok(k - 1):
+                quant(o - 2)
+            if k == 1:
                 quant_w(2)
                 quant_w(3)
-            if it == 4:
+            tf(e)
+            if k == 0:
+                const_bias_t()
+            tf(o)
+            if ok(k - 3):
+                aggr(k - 3)
+                sqrt(k - 3)
+            if ok(k - 4):
+                norm2(k - 4)
+            if ok(k - 3):
+                norm1(k - 3)
+                recip(k - 3)
+            if ok(k - 2):
+                tback(k - 2)
+            head = k < 2
+            evac(e, 0, False)
+            evac(e, 1, head)
+            if k == 0:
+                regroup_w(0, "v")
+                regroup_w(1, "s")
+                quant(e)
+                quant_w(0)
+                quant_w(1)
+                const_bias_c()
+            evac(o, 0, False)
+            evac(o, 1, head)
+            if k == 0:
+                regroup_w(2, "v")
+                regroup_w(3, "s")
+            if k > 0:
+                quant(e)
+            if k == 2:
                 const_gb()
-            if it % 2 == 1 and it >= 3:
-                mm(it - 3)
-                mm(it - 2)
-            ln_round(t0)
-            if 2 <= it < NSTEP - 1:
-                evac(it, 1, ev_on_vector(it))
-        quant(NSTEP - 1)
-        mm(NSTEP - 2)
-        mm(NSTEP - 1)
-        for s in range(NSTEP - 4, NSTEP):
-            relu(s)
-            if s == NSTEP - 4:
-                sqrt(NSTEP - L_TB - 1)
-        for a in range(NSTEP - L_TB, NSTEP + 3):
-            if rt(a):
-                tback(a)
-            ln_round(a)
-            if rt(a):
-                sqrt(a)
+            if ok(k - 1):
+                mm(e - 2)
+                mm(o - 2)
+            if k == NBLK - 1:
+                mm(e)
+            if ok(k - 2):
+                stats(k - 2)
+
+        L = NBLK - 1
+        relu(2 * L - 2)
+        relu(2 * L - 1)
+        quant(2 * L + 1)
+        mm(2 * L + 1)
+        aggr(L - 2)
+        sqrt(L - 2)
+        norm2(L - 3)
+        norm1(L - 2)
+        recip(L - 2)
+        tback(L - 1)
+        relu(2 * L)
+        relu(2 * L + 1)
+        tback(L)
+        stats(L - 1)
+        norm2(L - 2)
+        aggr(L - 1)
+        sqrt(L - 1)
+        stats(L)
+        norm1(L - 1)
+        recip(L - 1)
+        aggr(L)
+        sqrt(L)
+        norm2(L - 1)
+        norm1(L)
+        recip(L)
+        norm2(L)

@@ -22,6 +22,8 @@ XBUFS = 18
 AHEAD = 14
 V_EV = ()
 Q_LEAD = 3
+V_EVERY = 4
+HS_V = ()
 
 
 def tile_multiheadattentionunit_pa_t_kernel(tc, attn, Wo, bo, query_inputs, gamma, beta, out):
@@ -174,25 +176,34 @@ def tile_multiheadattentionunit_pa_t_kernel(tc, attn, Wo, bo, query_inputs, gamm
                         stop=(g == 1),
                     )
 
-        def relu(s):
-            h = s % 2
-            r = work.tile([P, 2, 256], F32, name="r", tag="r", bufs=6)
-            rs[s] = r
+        def relu(blk):
+            for h in range(2):
+                rs[2 * blk + h] = work.tile([P, 2, 256], F32, name="r%d" % h, tag="r%d" % h, bufs=3)
             for dh in (1, 0):
-                nc.scalar.activation(out=r[:, dh, :], in_=pps[s][:, dh, :], func=ACT.Relu,
-                                     bias=bias_f[:, 2 * h + dh:2 * h + dh + 1], scale=1.0)
+                for h in range(2):
+                    s = 2 * blk + h
+                    nc.scalar.activation(out=rs[s][:, dh, :], in_=pps[s][:, dh, :], func=ACT.Relu,
+                                         bias=bias_f[:, 2 * h + dh:2 * h + dh + 1], scale=1.0)
 
-        def tback(blk):
-            tb = psum.tile([P, 2, D], F32, name="tb", tag="tb", bufs=2)
+        def hsum(blk):
+            for dh in (1, 0):
+                eng = nc.vector if dh in HS_V else nc.gpsimd
+                eng.tensor_tensor(out=rs[2 * blk][:, dh, :], in0=rs[2 * blk][:, dh, :], in1=rs[2 * blk + 1][:, dh, :], op=ALU.add)
+
+        def tback(blk, heads):
+            if heads == 1:
+                tb = psum.tile([P, 2, D], F32, name="tb", tag="tb", bufs=2)
+            else:
+                tb = psum.tile([P, 2, D], F32, name="tb", tag="tf", bufs=4)
             tbs[blk] = tb
             nc.tensor.matmul(tb[:].rearrange("p j d -> p (j d)"), lhsT=ident_b[:],
                              rhs=qts[blk][:].rearrange("p j d -> p (j d)"), start=True, stop=False)
             for jj in range(2):
                 for dh in range(2):
-                    for h in range(2):
+                    for h in range(heads):
                         nc.tensor.matmul(tb[:, jj, dh * P:(dh + 1) * P], lhsT=rs[2 * blk + h][:, dh, jj * P:(jj + 1) * P],
                                          rhs=ident_f[:], is_transpose=True, start=False,
-                                         stop=(jj == 1 and dh == 1 and h == 1))
+                                         stop=(jj == 1 and dh == 1 and h == heads - 1))
 
         def stats(blk):
             st[blk] = dict(
@@ -253,9 +264,6 @@ def tile_multiheadattentionunit_pa_t_kernel(tc, attn, Wo, bo, query_inputs, gamm
                     loads_for(s)
                 elif s % 2 == 1 and ok((s - Q_LEAD) // 2):
                     load_q((s - Q_LEAD) // 2)
-            if ok(k - 2):
-                relu(e - 4)
-                relu(o - 4)
             if ok(k - 1):
                 quant(o - 2)
             if k == 1:
@@ -265,16 +273,15 @@ def tile_multiheadattentionunit_pa_t_kernel(tc, attn, Wo, bo, query_inputs, gamm
             if k == 0:
                 const_bias_t()
             tf(o)
+            if ok(k - 2):
+                hsum(k - 2)
+            if ok(k - 3):
+                stats(k - 3)
+            if ok(k - 4):
+                recip(k - 4)
+                norm1(k - 4)
             if ok(k - 3):
                 aggr(k - 3)
-                sqrt(k - 3)
-            if ok(k - 4):
-                norm2(k - 4)
-            if ok(k - 3):
-                norm1(k - 3)
-                recip(k - 3)
-            if ok(k - 2):
-                tback(k - 2)
             head = k < 2
             evac(e, 0, False)
             evac(e, 1, head)
@@ -286,46 +293,42 @@ def tile_multiheadattentionunit_pa_t_kernel(tc, attn, Wo, bo, query_inputs, gamm
                 quant_w(1)
                 const_bias_c()
             evac(o, 0, False)
-            evac(o, 1, head)
+            if ok(k - 3):
+                sqrt(k - 3)
+            evac(o, 1, head or k % V_EVERY == 1)
             if k == 0:
                 regroup_w(2, "v")
                 regroup_w(3, "s")
             if k > 0:
                 quant(e)
-            if k == 2:
-                const_gb()
+            if ok(k - 4):
+                norm2(k - 4)
             if ok(k - 1):
                 mm(e - 2)
                 mm(o - 2)
+            if k == 2:
+                const_gb()
+            if ok(k - 2):
+                tback(k - 2, 1)
             if k == NBLK - 1:
                 mm(e)
-            if ok(k - 2):
-                stats(k - 2)
+            if ok(k - 1):
+                relu(k - 1)
 
         L = NBLK - 1
-        relu(2 * L - 2)
-        relu(2 * L - 1)
         quant(2 * L + 1)
         mm(2 * L + 1)
-        aggr(L - 2)
-        sqrt(L - 2)
-        norm2(L - 3)
-        norm1(L - 2)
-        recip(L - 2)
-        tback(L - 1)
-        relu(2 * L)
-        relu(2 * L + 1)
-        tback(L)
-        stats(L - 1)
-        norm2(L - 2)
-        aggr(L - 1)
-        sqrt(L - 1)
-        stats(L)
-        norm1(L - 1)
-        recip(L - 1)
-        aggr(L)
-        sqrt(L)
-        norm2(L - 1)
-        norm1(L)
-        recip(L)
-        norm2(L)
+        tback(L - 1, 2)
+        relu(L)
+        tback(L, 2)
+        for b in range(L - 2, L + 3):
+            if ok(b):
+                stats(b)
+            if ok(b - 1):
+                recip(b - 1)
+                norm1(b - 1)
+            if ok(b):
+                aggr(b)
+                sqrt(b)
+            if ok(b - 1):
+                norm2(b - 1)

@@ -22,8 +22,8 @@ XBUFS = 18
 AHEAD = 14
 V_EV = ()
 Q_LEAD = 3
-V_EVERY = 4
-HS_V = ()
+V_EVERY = 100
+HS_VC = 128
 
 
 def tile_multiheadattentionunit_pa_t_kernel(tc, attn, Wo, bo, query_inputs, gamma, beta, out):
@@ -186,9 +186,12 @@ def tile_multiheadattentionunit_pa_t_kernel(tc, attn, Wo, bo, query_inputs, gamm
                                          bias=bias_f[:, 2 * h + dh:2 * h + dh + 1], scale=1.0)
 
         def hsum(blk):
-            for dh in (1, 0):
-                eng = nc.vector if dh in HS_V else nc.gpsimd
-                eng.tensor_tensor(out=rs[2 * blk][:, dh, :], in0=rs[2 * blk][:, dh, :], in1=rs[2 * blk + 1][:, dh, :], op=ALU.add)
+            a, b = rs[2 * blk], rs[2 * blk + 1]
+            if HS_VC > 0:
+                nc.vector.tensor_tensor(out=a[:, 1, 0:HS_VC], in0=a[:, 1, 0:HS_VC], in1=b[:, 1, 0:HS_VC], op=ALU.add)
+            if HS_VC < 256:
+                nc.gpsimd.tensor_tensor(out=a[:, 1, HS_VC:256], in0=a[:, 1, HS_VC:256], in1=b[:, 1, HS_VC:256], op=ALU.add)
+            nc.gpsimd.tensor_tensor(out=a[:, 0, :], in0=a[:, 0, :], in1=b[:, 0, :], op=ALU.add)
 
         def tback(blk, heads):
             if heads == 1:

@@ -124,9 +124,12 @@ def tile_multiheadattentionunit_pa_t_kernel(tc, attn, Wo, bo, query_inputs, gamm
         def const_bias_c():
             nc.vector.tensor_copy(out=bias_f[:], in_=bps[:, 0:4])
 
-        def const_gb():
-            cps = psum.tile([P, 2 * D], F32, name="cps", tag="tb", bufs=2)
+        cps = psum.tile([P, 2 * D], F32, name="cps", tag="tb", bufs=2)
+
+        def const_gb_m():
             nc.tensor.matmul(cps[:], lhsT=ones_b[:], rhs=gbrow[:], start=True, stop=True)
+
+        def const_gb_c():
             nc.vector.tensor_copy(out=gb[:], in_=cps[:])
 
         def tf(s):
@@ -275,6 +278,7 @@ def tile_multiheadattentionunit_pa_t_kernel(tc, attn, Wo, bo, query_inputs, gamm
             tf(e)
             if k == 0:
                 const_bias_t()
+                const_gb_m()
             tf(o)
             if ok(k - 2):
                 hsum(k - 2)
@@ -302,15 +306,17 @@ def tile_multiheadattentionunit_pa_t_kernel(tc, attn, Wo, bo, query_inputs, gamm
             if k == 0:
                 regroup_w(2, "v")
                 regroup_w(3, "s")
+                const_gb_c()
             if k > 0:
                 quant(e)
             if ok(k - 4):
                 norm2(k - 4)
-            if ok(k - 1):
+            if k == 0:
+                mm(e)
+            if k > 1:
                 mm(e - 2)
+            if k > 0:
                 mm(o - 2)
-            if k == 2:
-                const_gb()
             if ok(k - 2):
                 tback(k - 2, 1)
             if k == NBLK - 1:

@@ -23,7 +23,7 @@ AHEAD = 14
 V_EV = ()
 Q_LEAD = 3
 V_EVERY = 100
-HS_VC = 128
+HS_VC = 256
 
 
 def tile_multiheadattentionunit_pa_t_kernel(tc, attn, Wo, bo, query_inputs, gamma, beta, out):

from contextlib import ExitStack

import concourse.mybir as mybir
from concourse.masks import make_identity

F32 = mybir.dt.float32
BF16 = mybir.dt.bfloat16
U32 = mybir.dt.uint32
U8 = mybir.dt.uint8
FP8X4 = mybir.dt.float8_e4m3fn_x4
ALU = mybir.AluOpType
ACT = mybir.ActivationFunctionType

B, H, S, DV, D = 4, 2, 1024, 1024, 256
LN_EPS = 1e-3
FLOPS = 2 * B * H * S * DV * D

P = 128
NSTEP = 32
NBLK = 16
XBUFS = 18
AHEAD = 14
V_EV = ()
Q_LEAD = 3
V_EVERY = 100
HS_VC = 256


def tile_multiheadattentionunit_pa_t_kernel(tc, attn, Wo, bo, query_inputs, gamma, beta, out):
    nc = tc.nc
    with ExitStack() as ctx:
        const = ctx.enter_context(tc.tile_pool(name="const", bufs=1))
        xpool = ctx.enter_context(tc.tile_pool(name="xpool", bufs=XBUFS))
        work = ctx.enter_context(tc.tile_pool(name="work", bufs=3))
        stat = ctx.enter_context(tc.tile_pool(name="stat", bufs=6))
        psum = ctx.enter_context(tc.psum_pool(name="psum", bufs=1))
        ctx.enter_context(tc.manual_schedule())

        xin = {}
        grps = {}
        banks = {}
        codes = {}
        scls = {}
        pps = {}
        rs = {}
        tbs = {}
        ys = {}
        outs = {}
        st = {}
        qts = {}

        def load(s, parts):
            blk, h = s // 2, s % 2
            x = xpool.tile([P, 2, DV], BF16, name="xin", tag="xin")
            r0 = (blk % 4) * 256
            src = attn[blk // 4, h, r0:r0 + 256, :].rearrange("(p j) k -> p j k", j=2)
            w = DV // parts
            for i in range(parts):
                nc.sync.dma_start(out=x[:, :, i * w:(i + 1) * w], in_=src[:, :, i * w:(i + 1) * w])
            xin[s] = x

        def load_q(blk):
            qt = work.tile([P, 2, D], BF16, name="qt", tag="qt", bufs=10)
            r0 = (blk % 4) * 256
            nc.sync.dma_start(out=qt[:], in_=query_inputs[blk // 4, r0:r0 + 256, :].rearrange("(p j) d -> p j d", j=2))
            qts[blk] = qt

        load(0, 2)

        gbrow = const.tile([P, 2 * D], BF16, name="gbrow")
        nc.vector.memset(gbrow[:], 0.0)
        zb = const.tile([P, P], BF16, name="zb")
        nc.vector.memset(zb[:], 0.0)
        nc.scalar.dma_start(out=zb[0:4, :], in_=bo.rearrange("h (c p) -> (h c) p", p=P))
        nc.scalar.dma_start(out=gbrow[0:1, 0:D], in_=gamma.rearrange("(o d) -> o d", o=1))
        nc.scalar.dma_start(out=gbrow[0:1, D:2 * D], in_=beta.rearrange("(o d) -> o d", o=1))
        one_t = const.tile([P, 1], F32, name="one_t")
        nc.vector.memset(one_t[:], 1.0)
        eps_t = const.tile([P, 1], F32, name="eps_t")
        nc.vector.tensor_scalar(out=eps_t[:], in0=one_t[:], scalar1=LN_EPS, scalar2=None, op0=ALU.mult)
        scr = const.tile([P, 1], F32, name="scr")
        nc.scalar.activation(out=scr[:], in_=eps_t[:], func=ACT.Sqrt)
        ident_f = const.tile([P, P], F32, name="ident_f")
        make_identity(nc, ident_f[:])
        ident_b = const.tile([P, P], BF16, name="ident_b")
        make_identity(nc, ident_b[:])
        ones_b = const.tile([P, P], BF16, name="ones_b")
        nc.gpsimd.memset(ones_b[:], 1.0)

        wraw = const.tile([P, 4, 4, D], BF16, name="wraw")
        wcodes = const.tile([P, 4, D], U32, name="wcodes", align_bytes=64)
        wscl = const.tile([P, 4, D], U8, name="wscl", align_bytes=64)
        wgrp = const.tile([P, 4, D, 4], BF16, name="wgrp", align_bytes=64)
        gb = const.tile([P, 2 * D], F32, name="gb")
        bias_f = const.tile([P, 4], F32, name="bias_f")
        gam = gb[:, 0:D]
        bet = gb[:, D:2 * D]

        def load_w(h):
            nc.sync.dma_start(
                out=wraw[:, 2 * h:2 * h + 2, :, :].rearrange("p a t c -> p (a t c)").rearrange("p (x y) -> p x y", y=2 * D),
                in_=Wo[h].rearrange("(g u p e) c -> p (g u) (e c)", g=2, u=2, p=P, e=2),
            )

        def regroup_w(a, eng):
            src = wraw[:, a, :, :].rearrange("p t c -> p c t")
            if eng == "v":
                nc.vector.tensor_copy(out=wgrp[:, a, :, :], in_=src)
            else:
                nc.scalar.copy(out=wgrp[:, a, :, :], in_=src)

        def quant_w(a):
            nc.vector.quantize_mx(
                out=wcodes[:, a, :].bitcast(FP8X4),
                scales=wscl[:, a, :],
                in_=wgrp[:, a, :, :].rearrange("p c t -> p (c t)"),
            )

        bps = psum.tile([P, P], BF16, name="bps", tag="tb", bufs=2)

        def const_bias_t():
            nc.tensor.transpose(bps[:], zb[:], ident_b[:])

        def const_bias_c():
            nc.vector.tensor_copy(out=bias_f[:], in_=bps[:, 0:4])

        cps = psum.tile([P, 2 * D], F32, name="cps", tag="tb", bufs=2)

        def const_gb_m():
            nc.tensor.matmul(cps[:], lhsT=ones_b[:], rhs=gbrow[:], start=True, stop=True)

        def const_gb_c():
            nc.vector.tensor_copy(out=gb[:], in_=cps[:])

        def tf(s):
            grps[s] = work.tile([P, 512, 2], F32, name="grp", tag="grp", bufs=4, align_bytes=64)
            for g in range(2):
                bank = psum.tile([P, 2, 2, P], F32, name="tf", tag="tf", bufs=4)
                banks[(s, g)] = bank
                for u in range(2):
                    for jj in range(2):
                        c0 = 256 * g + 128 * u
                        nc.tensor.transpose(bank[:, u, jj, :], xin[s][:, jj, :].bitcast(F32)[:, c0:c0 + 128], ident_f[:])

        def evac(s, g, on_vector):
            src = banks[(s, g)][:].rearrange("p u j r -> p (j r) u")
            dst = grps[s][:, g * 256:(g + 1) * 256, :]
            if on_vector:
                nc.vector.tensor_copy(out=dst, in_=src)
            else:
                nc.scalar.copy(out=dst, in_=src)

        def quant(s):
            ac = work.tile([P, 512], U32, name="ac", tag="ac", bufs=5, align_bytes=64)
            asc = work.tile([P, 512], U8, name="asc", tag="asc", bufs=5, align_bytes=64)
            nc.vector.quantize_mx(
                out=ac[:].bitcast(FP8X4),
                scales=asc[:],
                in_=grps[s][:].rearrange("p c u -> p (c u)").bitcast(BF16),
            )
            codes[s] = ac
            scls[s] = asc

        def mm(s):
            h = s % 2
            if s >= NSTEP - 2:
                pps[s] = psum.tile([P, 2, 256], F32, name="pp", tag="tf", bufs=4)
            else:
                pps[s] = psum.tile([P, 2, 256], F32, name="pp", tag="pp", bufs=2)
            for dh in range(2):
                for g in range(2):
                    nc.tensor.matmul_mx(
                        out=pps[s][:, dh, :],
                        lhsT=wcodes[:, 2 * h + g, dh * P:(dh + 1) * P].bitcast(FP8X4),
                        lhsT_scale=wscl[:, 2 * h + g, dh * P:(dh + 1) * P],
                        rhs=codes[s][:, g * 256:(g + 1) * 256].bitcast(FP8X4),
                        rhs_scale=scls[s][:, g * 256:(g + 1) * 256],
                        start=(g == 0),
                        stop=(g == 1),
                    )

        def relu(blk):
            for h in range(2):
                rs[2 * blk + h] = work.tile([P, 2, 256], F32, name="r%d" % h, tag="r%d" % h, bufs=3)
            for dh in (1, 0):
                for h in range(2):
                    s = 2 * blk + h
                    nc.scalar.activation(out=rs[s][:, dh, :], in_=pps[s][:, dh, :], func=ACT.Relu,
                                         bias=bias_f[:, 2 * h + dh:2 * h + dh + 1], scale=1.0)

        def hsum(blk):
            a, b = rs[2 * blk], rs[2 * blk + 1]
            if HS_VC > 0:
                nc.vector.tensor_tensor(out=a[:, 1, 0:HS_VC], in0=a[:, 1, 0:HS_VC], in1=b[:, 1, 0:HS_VC], op=ALU.add)
            if HS_VC < 256:
                nc.gpsimd.tensor_tensor(out=a[:, 1, HS_VC:256], in0=a[:, 1, HS_VC:256], in1=b[:, 1, HS_VC:256], op=ALU.add)
            nc.gpsimd.tensor_tensor(out=a[:, 0, :], in0=a[:, 0, :], in1=b[:, 0, :], op=ALU.add)

        def tback(blk, heads):
            if heads == 1:
                tb = psum.tile([P, 2, D], F32, name="tb", tag="tb", bufs=2)
            else:
                tb = psum.tile([P, 2, D], F32, name="tb", tag="tf", bufs=4)
            tbs[blk] = tb
            nc.tensor.matmul(tb[:].rearrange("p j d -> p (j d)"), lhsT=ident_b[:],
                             rhs=qts[blk][:].rearrange("p j d -> p (j d)"), start=True, stop=False)
            for jj in range(2):
                for dh in range(2):
                    for h in range(heads):
                        nc.tensor.matmul(tb[:, jj, dh * P:(dh + 1) * P], lhsT=rs[2 * blk + h][:, dh, jj * P:(jj + 1) * P],
                                         rhs=ident_f[:], is_transpose=True, start=False,
                                         stop=(jj == 1 and dh == 1 and h == heads - 1))

        def stats(blk):
            st[blk] = dict(
                bn=stat.tile([P, 2, 6], F32, name="bn", tag="bn"),
                mv=stat.tile([P, 2, 2], F32, name="mv", tag="mv"),
                sd=stat.tile([P, 2], F32, name="sd", tag="sd"),
                rstd=stat.tile([P, 2], F32, name="rstd", tag="rstd"),
            )
            for jj in (1, 0):
                nc.vector.bn_stats(out=st[blk]["bn"][:, jj, :], in_=tbs[blk][:, jj, :])

        def aggr(blk):
            for jj in (1, 0):
                nc.vector.bn_aggr(out=st[blk]["mv"][:, jj, :], in_=st[blk]["bn"][:, jj, :])

        def sqrt(blk):
            nc.scalar.activation(out=st[blk]["sd"][:], in_=st[blk]["mv"][:, :, 1], func=ACT.Sqrt, bias=eps_t[:, 0:1], scale=1.0)

        def recip(blk):
            nc.vector.reciprocal(out=st[blk]["rstd"][:], in_=st[blk]["sd"][:])

        def norm1(blk):
            ys[blk] = work.tile([P, 2, D], F32, name="y", tag="y", bufs=3)
            for jj in range(2):
                nc.vector.scalar_tensor_tensor(out=ys[blk][:, jj, :], in0=tbs[blk][:, jj, :], scalar=st[blk]["mv"][:, jj, 0:1],
                                               in1=gam, op0=ALU.subtract, op1=ALU.mult)

        def norm2(blk):
            o = work.tile([P, 2, D], F32, name="o", tag="o", bufs=8)
            r0 = (blk % 4) * 256
            dst = out[blk // 4, r0:r0 + 256, :].rearrange("(p j) d -> p j d", j=2)
            for jj in range(2):
                nc.vector.scalar_tensor_tensor(out=o[:, jj, :], in0=ys[blk][:, jj, :], scalar=st[blk]["rstd"][:, jj:jj + 1],
                                               in1=bet, op0=ALU.mult, op1=ALU.add)
                if blk == NBLK - 1:
                    nc.sync.dma_start(out=dst[:, jj:jj + 1, :], in_=o[:, jj:jj + 1, :])
            if blk < NBLK - 1:
                nc.sync.dma_start(out=dst, in_=o[:])

        def ok(b):
            return 0 <= b < NBLK

        def loads_for(s):
            load(s, 1)
            if s % 2 == 1 and ok((s - Q_LEAD) // 2):
                load_q((s - Q_LEAD) // 2)

        load_w(0)
        load(1, 1)
        load_w(1)
        for s in range(2, AHEAD):
            loads_for(s)

        for k in range(NBLK):
            e, o = 2 * k, 2 * k + 1
            for s in (e + AHEAD, o + AHEAD):
                if s < NSTEP:
                    loads_for(s)
                elif s % 2 == 1 and ok((s - Q_LEAD) // 2):
                    load_q((s - Q_LEAD) // 2)
            if ok(k - 1):
                quant(o - 2)
            if k == 1:
                quant_w(2)
                quant_w(3)
            tf(e)
            if k == 0:
                const_bias_t()
                const_gb_m()
            tf(o)
            if ok(k - 2):
                hsum(k - 2)
            if ok(k - 3):
                stats(k - 3)
            if ok(k - 4):
                recip(k - 4)
                norm1(k - 4)
            if ok(k - 3):
                aggr(k - 3)
            head = k < 2
            evac(e, 0, False)
            evac(e, 1, head)
            if k == 0:
                regroup_w(0, "v")
                regroup_w(1, "s")
                quant(e)
                quant_w(0)
                quant_w(1)
                const_bias_c()
            evac(o, 0, False)
            if ok(k - 3):
                sqrt(k - 3)
            evac(o, 1, head or k % V_EVERY == 1)
            if k == 0:
                regroup_w(2, "v")
                regroup_w(3, "s")
                const_gb_c()
            if k > 0:
                quant(e)
            if ok(k - 4):
                norm2(k - 4)
            if k == 0:
                mm(e)
            if k > 1:
                mm(e - 2)
            if k > 0:
                mm(o - 2)
            if ok(k - 2):
                tback(k - 2, 1)
            if k == NBLK - 1:
                mm(e)
            if ok(k - 1):
                relu(k - 1)

        L = NBLK - 1
        quant(2 * L + 1)
        mm(2 * L + 1)
        tback(L - 1, 2)
        relu(L)
        tback(L, 2)
        for b in range(L - 2, L + 3):
            if ok(b):
                stats(b)
            if ok(b - 1):
                recip(b - 1)
                norm1(b - 1)
            if ok(b):
                aggr(b)
                sqrt(b)
            if ok(b - 1):
                norm2(b - 1)
